import numpy as np
import ml_dtypes


def mxq(x, axis, fmt="e4m3"):
    dtype, down = {"e4m3": (ml_dtypes.float8_e4m3fn, 7), "e5m2": (ml_dtypes.float8_e5m2, 14)}[fmt]
    v = np.moveaxis(np.asarray(x, np.float32).astype(ml_dtypes.bfloat16).astype(np.float64), axis, -1)
    blocks = v.reshape(v.shape[:-1] + (-1, 32))
    amax = np.abs(blocks).max(-1, keepdims=True)
    byte = np.maximum(np.where(amax > 0, np.frexp(amax)[1] - 1 + 127, 0) - down, 1)
    scale = np.exp2(byte - 127.0)
    codes = (blocks / scale).astype(np.float32).astype(dtype).astype(np.float64)
    return np.moveaxis((codes * scale).reshape(v.shape), -1, axis)


WIDE = False


def mx_kscale(k):
    if not WIDE:
        return np.ones(k)
    levels = np.array([10, -10, 5, -5, 0])
    a = np.random.permutation(np.resize(levels, k // 512 * 4)).reshape(k // 512, 4)
    idx = np.arange(k)
    return np.exp2(a[idx // 512, idx % 128 // 32])


BF16 = ml_dtypes.bfloat16


def bf(x):
    return np.asarray(x, np.float32).astype(BF16)


def f64(x):
    return np.asarray(x).astype(np.float64)


B, V, R = 4096, 1024, 512

ALPHA = 0.3


def setup_inputs():
    s = mx_kscale(V)
    return {"logits": bf(np.random.standard_normal((B, V)) * s / s.max()),
            "W": bf(np.random.standard_normal((V, R)) * 2.0 * (B / R) ** 0.25 / s[:, None])}


def reference(logits, W):
    logits, W = f64(logits), f64(W)
    l_n = np.linalg.norm(logits)
    logits_n = logits / l_n
    h = mxq(logits_n, 1, "e4m3") @ mxq(W, 0, "e4m3")
    minted = mxq(h, 1, "e4m3") @ mxq(W, 1, "e4m3").T
    minted = minted / np.linalg.norm(minted)
    out = (1.0 - ALPHA) * minted + ALPHA * logits_n
    out = out / np.linalg.norm(out) * l_n
    return out

@@ -1,0 +1,357 @@
+from contextlib import ExitStack
+
+import concourse.mybir as mybir
+from concourse.masks import make_identity
+
+FP8X4 = mybir.dt.float8_e4m3fn_x4
+BF16 = mybir.dt.bfloat16
+F32 = mybir.dt.float32
+U32 = mybir.dt.uint32
+U8 = mybir.dt.uint8
+ALU = mybir.AluOpType
+ACT = mybir.ActivationFunctionType
+AX = mybir.AxisListType
+
+P = 128
+B, V, R = 4096, 1024, 512
+ALPHA = 0.3
+FLOPS = 2 * B * V * R * 2
+
+NT = B // P
+CHUNK = 4
+NCHUNK = NT // CHUNK
+BANK = 512
+PIECES = NT * V // BANK
+TILE_WORDS = V // 4
+SLAB = V // 4
+R2 = R // 2
+
+GRAM_TILES = [2, 2, 2, 2, 2, 2, 2, 3]
+SQ_COLS = 16
+EARLY_CHUNKS = 6
+EARLY_BANKS = 7
+LATE_BANKS = [3, 4, 5, 6]
+
+UNITS = [(0, 1), (1, 1)] + [(t, 2) for t in range(2, NT, 2)]
+NU = len(UNITS)
+VECTOR_SCALED = 5
+H_BANKS = [0, 1, 2]
+M_BANKS = [7, 3, 4, 5, 6]
+
+STORE_PIECES = [1, 1, 2] + [4] * 14 + [2, 1, 1]
+
+
+def tile_lowrankredistributor_t_kernel(tc, logits, W, out):
+    nc = tc.nc
+    x_rows = logits.rearrange("(p t) v -> p t v", t=NT)
+    out_rows = out.rearrange("(p t) v -> p (t v)", t=NT)
+    cross = 2.0 * ALPHA * (1.0 - ALPHA)
+    with ExitStack() as ctx:
+        ctx.enter_context(tc.manual_schedule())
+        keep = ctx.enter_context(tc.tile_pool(name="keep", bufs=1))
+        psum = ctx.enter_context(tc.psum_pool(name="psum", bufs=1))
+
+        def bank(index, shape, dtype, name):
+            return psum.tile(shape, dtype, tag="b%d" % index, name=name)
+
+        warm = keep.tile([P, 1], F32)
+        nc.vector.memset(warm[:], 1.0)
+        nc.scalar.activation(out=warm[:], in_=warm[:], func=ACT.Sqrt)
+        ident = keep.tile([P, P], F32)
+        make_identity(nc, ident[:])
+        ones = keep.tile([P, P], F32)
+        nc.vector.memset(ones[:], 1.0)
+
+        x_sb = keep.tile([P, NT, V], BF16)
+        x_words = x_sb[:].bitcast(F32)
+        w0_codes = keep.tile([P, 2 * R], U32, align_bytes=64)
+        w0_scales = keep.tile([P, 2 * R], U8, align_bytes=64)
+        wt_codes = keep.tile([P, V], U32, align_bytes=64)
+        wt_scales = keep.tile([P, V], U8, align_bytes=64)
+        h_codes = keep.tile([P, B], U32, align_bytes=64)
+        h_scales = keep.tile([P, B], U8, align_bytes=64)
+        sq_gram = keep.tile([P, SQ_COLS], F32)
+        nc.vector.memset(sq_gram[:], 0.0)
+        sq_scalar = keep.tile([P, SQ_COLS], F32)
+        nc.vector.memset(sq_scalar[:], 0.0)
+        m_sums = keep.tile([P, 2, PIECES], F32)
+        sum_x2 = keep.tile([P, 1], F32)
+        l_n = keep.tile([P, 1], F32)
+        inv_l_n = keep.tile([P, 1], F32)
+        inv_l_n_gp = keep.tile([P, 1], F32)
+        totals = keep.tile([P, 2], F32)
+        m_norm = keep.tile([P, 1], F32)
+        denom = keep.tile([P, 1], F32)
+        inv_denom = keep.tile([P, 1], F32)
+        rho = keep.tile([P, 1], F32)
+        o_sq = keep.tile([P, 1], F32)
+        o_norm = keep.tile([P, 1], F32)
+        beta = keep.tile([P, 1], F32)
+        rho_beta = keep.tile([P, 1], F32)
+
+        def x_piece(piece):
+            return x_sb[:, piece // 2, (piece % 2) * BANK:(piece % 2 + 1) * BANK]
+
+        def second_matmul(piece, index):
+            t = piece // 2
+            cols = slice((piece % 2) * BANK, (piece % 2 + 1) * BANK)
+            minted = bank(index, [P, BANK], F32, "minted")
+            nc.tensor.matmul_mx(
+                out=minted[:],
+                lhsT=h_codes[:, t * P:(t + 1) * P].bitcast(FP8X4),
+                lhsT_scale=h_scales[:, t * P:(t + 1) * P],
+                rhs=wt_codes[:, cols].bitcast(FP8X4),
+                rhs_scale=wt_scales[:, cols],
+                start=True, stop=True)
+            return minted
+
+        with tc.tile_pool(name="ab", bufs=1) as ab:
+            w_raw = ab.tile([P, 4, 2, R], BF16)
+            w_raw_words = w_raw[:].bitcast(F32)
+            w_by_pass = w_raw[:].rearrange("q (g u) e r -> q g (u e) r", g=2)
+            xt_words = ab.tile([P, NT, V // 2], F32, align_bytes=64)
+            xt = xt_words[:].bitcast(BF16)
+            w0_grouped = ab.tile([P, 2, R, 4], BF16, align_bytes=64)
+            wt_grouped = ab.tile([P, V, 2], F32, align_bytes=64)
+
+            nc.sync.dma_start(out=x_sb[:, 0:2, :], in_=x_rows[:, 0:2, :])
+            nc.sync.dma_start(out=x_sb[:, 2:4, :], in_=x_rows[:, 2:4, :])
+            nc.sync.dma_start(out=x_sb[:, 4:8, :], in_=x_rows[:, 4:8, :])
+            nc.sync.dma_start(out=w_raw[:], in_=W.rearrange("(s q e) r -> q s e r", s=4, e=2))
+            for c in range(2, NCHUNK):
+                nc.sync.dma_start(out=x_sb[:, c * CHUNK:(c + 1) * CHUNK, :],
+                                  in_=x_rows[:, c * CHUNK:(c + 1) * CHUNK, :])
+
+            gram = bank(7, [P, P], F32, "gram")
+            gram_tiles = [c * CHUNK + i for c in range(NCHUNK) for i in range(GRAM_TILES[c])]
+            xt_bank = {}
+
+            def square_on_tensor(t):
+                for j in range(V // P):
+                    block = x_sb[:, t, j * P:(j + 1) * P]
+                    nc.tensor.matmul(out=gram[:], lhsT=block, rhs=block, start=(t == gram_tiles[0] and j == 0),
+                                     stop=(t == gram_tiles[-1] and j == V // P - 1))
+
+            def square_on_scalar(t, col):
+                squares = ab.tile([P, V], BF16, bufs=2, name="squares")
+                nc.scalar.activation(out=squares[:], in_=x_sb[:, t, :], func=ACT.Square,
+                                     accum_out=sq_scalar[:, col:col + 1])
+
+            def transpose_x(t, index):
+                xt_bank[t] = bank(index, [P, 4, P], F32, "xt_bank")
+                for gu in range(4):
+                    nc.tensor.transpose(out=xt_bank[t][:, gu, :], in_=x_words[:, t, gu * P:(gu + 1) * P],
+                                        identity=ident[:])
+
+            def copy_out_x(t, engine):
+                dst = xt_words[:, t, :].rearrange("q (g n u) -> q g n u", g=2, u=2)
+                src = xt_bank[t][:].rearrange("q (g u) n -> q g n u", g=2)
+                if engine == "scalar":
+                    nc.scalar.copy(out=dst, in_=src)
+                else:
+                    nc.vector.tensor_copy(out=dst, in_=src)
+
+            def regroup_w0(g, u2):
+                nc.vector.tensor_copy(
+                    out=w0_grouped[:, g, u2 * R2:(u2 + 1) * R2, :].rearrange("q (e p) y -> q e p y", e=2),
+                    in_=w_by_pass[:, g, :, u2 * R2:(u2 + 1) * R2].rearrange("q y (p e) -> q e p y", e=2))
+
+            def transpose_w(s, index):
+                wt_bank = bank(index, [P, 2, 2, P], F32, "wt_bank")
+                for e in range(2):
+                    for u in range(2):
+                        nc.tensor.transpose(out=wt_bank[:, e, u, :], in_=w_raw_words[:, s, e, u * P:(u + 1) * P],
+                                            identity=ident[:])
+                nc.scalar.copy(out=wt_grouped[:, s * SLAB:(s + 1) * SLAB, :].rearrange("p (q e) u -> p q e u", e=2),
+                               in_=wt_bank[:].rearrange("p e u q -> p q e u"))
+
+            turn = 0
+            col = 0
+            for c in range(NCHUNK):
+                tiles = list(range(c * CHUNK, (c + 1) * CHUNK))
+                for t in tiles[GRAM_TILES[c]:]:
+                    square_on_scalar(t, col)
+                    col += 1
+                for t in tiles[:GRAM_TILES[c]]:
+                    square_on_tensor(t)
+                if c < EARLY_CHUNKS:
+                    for t in tiles:
+                        transpose_x(t, turn % EARLY_BANKS)
+                        turn += 1
+                        copy_out_x(t, "vector")
+                if c == 1:
+                    for g in range(2):
+                        for u2 in range(2):
+                            regroup_w0(g, u2)
+                if c == 1 or c == 2:
+                    for s in (2 * c - 2, 2 * c - 1):
+                        transpose_w(s, turn % EARLY_BANKS)
+                        turn += 1
+                if c == 2:
+                    nc.vector.quantize_mx(out=w0_codes[:].bitcast(FP8X4), scales=w0_scales[:],
+                                          in_=w0_grouped[:].rearrange("q g r y -> q (g r y)"))
+                if c == 3:
+                    nc.vector.quantize_mx(out=wt_codes[:].bitcast(FP8X4), scales=wt_scales[:],
+                                          in_=wt_grouped[:].bitcast(BF16).rearrange("p v y -> p (v y)"))
+
+            late = list(range(EARLY_CHUNKS * CHUNK, NT))
+            for i, t in enumerate(late[:3]):
+                transpose_x(t, LATE_BANKS[i % 4])
+            diagonal = ab.tile([P, P], F32)
+            nc.vector.scalar_tensor_tensor(out=diagonal[:], in0=gram[:], scalar=1.0, in1=ident[:],
+                                           op0=ALU.mult, op1=ALU.mult, accum_out=sq_gram[:, 0:1])
+            copy_out_x(late[0], "vector")
+            copy_out_x(late[1], "scalar")
+            copy_out_x(late[2], "vector")
+            x2_bank = bank(7, [P, 2 * SQ_COLS], F32, "x2_bank")
+            nc.tensor.matmul(out=x2_bank[:, 0:SQ_COLS], lhsT=ones[:], rhs=sq_gram[:], start=True, stop=True)
+            nc.tensor.matmul(out=x2_bank[:, SQ_COLS:2 * SQ_COLS], lhsT=ones[:], rhs=sq_scalar[:],
+                             start=True, stop=True)
+            for i, t in enumerate(late[3:]):
+                transpose_x(t, LATE_BANKS[(i + 3) % 4])
+            nc.vector.reduce_sum(out=sum_x2[:], in_=x2_bank[:], axis=AX.X)
+            nc.scalar.activation(out=l_n[:], in_=sum_x2[:], func=ACT.Sqrt)
+            nc.vector.reciprocal(out=inv_l_n[:], in_=l_n[:])
+            waiting = late[3:]
+
+            xs = {}
+            xq = {}
+            hg = {}
+
+            def new_xs(unit):
+                xs[unit] = ab.tile([P, UNITS[unit][1] * V], BF16, align_bytes=64, bufs=3, name="xs", tag="xs")
+
+            def scale_x(unit, engine):
+                t0, nt = UNITS[unit]
+                src = xt[:, t0:t0 + nt, :].rearrange("q t v -> q (t v)")
+                if engine == "gpsimd":
+                    nc.gpsimd.tensor_scalar(out=xs[unit][:], in0=src, scalar1=inv_l_n_gp[:, 0:1], scalar2=0.0,
+                                            op0=ALU.mult, op1=ALU.add)
+                else:
+                    nc.vector.tensor_scalar(out=xs[unit][:], in0=src, scalar1=inv_l_n[:, 0:1], scalar2=None,
+                                            op0=ALU.mult)
+
+            def quantise_x(unit):
+                nt = UNITS[unit][1]
+                codes = ab.tile([P, nt * TILE_WORDS], U32, align_bytes=64, bufs=3, name="xq", tag="xq")
+                scales = ab.tile([P, nt * TILE_WORDS], U8, align_bytes=64, bufs=3, name="xqs", tag="xqs")
+                nc.vector.quantize_mx(out=codes[:].bitcast(FP8X4), scales=scales[:], in_=xs[unit][:])
+                xq[unit] = (codes, scales)
+
+            def first_matmul(unit):
+                t0, nt = UNITS[unit]
+                codes, scales = xq[unit]
+                hg[unit] = ab.tile([P, nt, P, 4], BF16, align_bytes=64, bufs=3, name="hg", tag="hg")
+                for i in range(nt):
+                    h_bank = bank(H_BANKS[(t0 + i) % 3], [P, 4, P], F32, "h_bank")
+                    for y in range(4):
+                        for g in range(2):
+                            w_cols = slice(g * R + y * P, g * R + (y + 1) * P)
+                            x_cols = slice(i * TILE_WORDS + g * P, i * TILE_WORDS + (g + 1) * P)
+                            nc.tensor.matmul_mx(
+                                out=h_bank[:, y, :],
+                                lhsT=w0_codes[:, w_cols].bitcast(FP8X4),
+                                lhsT_scale=w0_scales[:, w_cols],
+                                rhs=codes[:, x_cols].bitcast(FP8X4),
+                                rhs_scale=scales[:, x_cols],
+                                start=(g == 0), stop=(g == 1))
+                    nc.scalar.copy(out=hg[unit][:, i], in_=h_bank[:].rearrange("p y n -> p n y"))
+
+            def quantise_h(unit):
+                t0, nt = UNITS[unit]
+                nc.vector.quantize_mx(out=h_codes[:, t0 * P:(t0 + nt) * P].bitcast(FP8X4),
+                                      scales=h_scales[:, t0 * P:(t0 + nt) * P],
+                                      in_=hg[unit][:].rearrange("p t n y -> p (t n y)"))
+
+            def sums_of_minted(unit):
+                t0, nt = UNITS[unit]
+                for piece in range(2 * t0, 2 * (t0 + nt)):
+                    minted = second_matmul(piece, M_BANKS[piece % 5])
+                    squares_m = ab.tile([P, BANK], BF16, bufs=2, name="squares_m")
+                    nc.scalar.activation(out=squares_m[:], in_=minted[:], func=ACT.Square,
+                                         accum_out=m_sums[:, 0, piece:piece + 1])
+                    products = ab.tile([P, BANK], F32, bufs=2, name="products")
+                    nc.vector.scalar_tensor_tensor(out=products[:], in0=minted[:], scalar=1.0, in1=x_piece(piece),
+                                                   op0=ALU.mult, op1=ALU.mult,
+                                                   accum_out=m_sums[:, 1, piece:piece + 1])
+
+            new_xs(0)
+            scale_x(0, "vector")
+            for i in range(-3, NU):
+                if i + 4 < VECTOR_SCALED:
+                    new_xs(i + 4)
+                    scale_x(i + 4, "vector")
+                if VECTOR_SCALED <= i + 5 < NU:
+                    new_xs(i + 5)
+                if i + 3 < NU:
+                    quantise_x(i + 3)
+                if i + 5 == VECTOR_SCALED:
+                    nc.vector.tensor_copy(out=inv_l_n_gp[:], in_=inv_l_n[:])
+                if 0 <= i + 1 < NU:
+                    quantise_h(i + 1)
+                if VECTOR_SCALED <= i + 5 < NU:
+                    scale_x(i + 5, "gpsimd")
+                if i >= 0:
+                    sums_of_minted(i)
+                if 0 <= i + 2 < NU:
+                    first_matmul(i + 2)
+                for t in waiting[:2]:
+                    copy_out_x(t, "scalar")
+                waiting = waiting[2:]
+
+        sums_bank = bank(0, [P, 2, PIECES], F32, "sums_bank")
+        nc.tensor.matmul(out=sums_bank[:].rearrange("p a k -> p (a k)"), lhsT=ones[:],
+                         rhs=m_sums[:].rearrange("p a k -> p (a k)"), start=True, stop=True)
+        nc.vector.reduce_sum(out=totals[:], in_=sums_bank[:], axis=AX.X)
+        nc.scalar.activation(out=m_norm[:], in_=totals[:, 0:1], func=ACT.Sqrt)
+        nc.vector.tensor_scalar(out=denom[:], in0=m_norm[:], scalar1=l_n[:, 0:1], scalar2=1.0 / cross,
+                                op0=ALU.mult, op1=ALU.mult)
+        nc.vector.reciprocal(out=inv_denom[:], in_=denom[:])
+        nc.vector.tensor_scalar(out=rho[:], in0=inv_denom[:], scalar1=sum_x2[:, 0:1],
+                                scalar2=(1.0 - ALPHA) / (ALPHA * cross), op0=ALU.mult, op1=ALU.mult)
+        nc.vector.tensor_scalar(out=o_sq[:], in0=totals[:, 1:2], scalar1=inv_denom[:, 0:1],
+                                scalar2=ALPHA * ALPHA + (1.0 - ALPHA) * (1.0 - ALPHA), op0=ALU.mult, op1=ALU.add)
+        nc.scalar.activation(out=o_norm[:], in_=o_sq[:], func=ACT.Sqrt, scale=1.0 / (ALPHA * ALPHA))
+
+        with tc.tile_pool(name="cc", bufs=1) as cc:
+            first = 0
+            fours = 0
+            for n_pieces in STORE_PIECES:
+                stage = cc.tile([P, n_pieces * BANK], F32, bufs=6, name="stage", tag="stage")
+                other_way = 0
+                beta_on_gpsimd = 0
+                if n_pieces == 4:
+                    if fours % 3 < 2:
+                        other_way = 1
+                    else:
+                        beta_on_gpsimd = 2
+                    fours += 1
+                on_vector = n_pieces - other_way
+                for i in range(n_pieces):
+                    piece = first + i
+                    cols = slice(i * BANK, (i + 1) * BANK)
+                    minted = second_matmul(piece, (piece + 1) % 8)
+                    if i < on_vector:
+                        nc.vector.scalar_tensor_tensor(out=stage[:, cols], in0=minted[:], scalar=rho[:, 0:1],
+                                                       in1=x_piece(piece), op0=ALU.mult, op1=ALU.add)
+                        if piece == 0:
+                            nc.vector.reciprocal(out=beta[:], in_=o_norm[:])
+                            nc.vector.tensor_scalar(out=rho_beta[:], in0=rho[:], scalar1=beta[:, 0:1], scalar2=None,
+                                                    op0=ALU.mult)
+                    else:
+                        beta_logits = cc.tile([P, BANK], F32, bufs=3, name="beta_logits", tag="beta_logits")
+                        nc.gpsimd.tensor_scalar(out=beta_logits[:], in0=x_piece(piece), scalar1=beta[:, 0:1],
+                                                scalar2=0.0, op0=ALU.mult, op1=ALU.add)
+                        nc.scalar.activation(out=stage[:, cols], in_=minted[:], func=ACT.Copy,
+                                             scale=rho_beta[:, 0:1])
+                        nc.gpsimd.tensor_tensor(out=stage[:, cols], in0=stage[:, cols], in1=beta_logits[:],
+                                                op=ALU.add)
+                on_scalar = slice(0, (on_vector - beta_on_gpsimd) * BANK)
+                nc.scalar.activation(out=stage[:, on_scalar], in_=stage[:, on_scalar], func=ACT.Copy,
+                                     scale=beta[:, 0:1])
+                if beta_on_gpsimd:
+                    rest = slice((on_vector - beta_on_gpsimd) * BANK, on_vector * BANK)
+                    nc.gpsimd.tensor_scalar(out=stage[:, rest], in0=stage[:, rest], scalar1=beta[:, 0:1],
+                                            scalar2=0.0, op0=ALU.mult, op1=ALU.add)
+                nc.sync.dma_start(out=out_rows[:, first * BANK:(first + n_pieces) * BANK], in_=stage[:])
+                first += n_pieces

@@ -18,23 +18,22 @@ ALPHA = 0.3
 FLOPS = 2 * B * V * R * 2
 
 NT = B // P
-CHUNK = 4
-NCHUNK = NT // CHUNK
 BANK = 512
 PIECES = NT * V // BANK
 TILE_WORDS = V // 4
 SLAB = V // 4
 R2 = R // 2
 
-GRAM_TILES = [2, 2, 2, 2, 2, 2, 2, 3]
-SQ_COLS = 16
-EARLY_CHUNKS = 6
+LOADS = [1, 1, 2, 4, 4, 4, 4, 4, 4, 2, 1, 1]
+SQUARES = "TTSS" * 8
+SQ_COLS = 32
+EARLY = 24
 EARLY_BANKS = 7
 LATE_BANKS = [3, 4, 5, 6]
 
 UNITS = [(0, 1), (1, 1)] + [(t, 2) for t in range(2, NT, 2)]
 NU = len(UNITS)
-VECTOR_SCALED = 5
+VECTOR_SCALED = 6
 H_BANKS = [0, 1, 2]
 M_BANKS = [7, 3, 4, 5, 6]
 
@@ -70,10 +69,8 @@ def tile_lowrankredistributor_t_kernel(tc, logits, W, out):
         wt_scales = keep.tile([P, V], U8, align_bytes=64)
         h_codes = keep.tile([P, B], U32, align_bytes=64)
         h_scales = keep.tile([P, B], U8, align_bytes=64)
-        sq_gram = keep.tile([P, SQ_COLS], F32)
-        nc.vector.memset(sq_gram[:], 0.0)
-        sq_scalar = keep.tile([P, SQ_COLS], F32)
-        nc.vector.memset(sq_scalar[:], 0.0)
+        sq_sums = keep.tile([P, SQ_COLS], F32)
+        nc.vector.memset(sq_sums[:], 0.0)
         m_sums = keep.tile([P, 2, PIECES], F32)
         sum_x2 = keep.tile([P, 1], F32)
         l_n = keep.tile([P, 1], F32)
@@ -81,8 +78,10 @@ def tile_lowrankredistributor_t_kernel(tc, logits, W, out):
         inv_l_n_gp = keep.tile([P, 1], F32)
         totals = keep.tile([P, 2], F32)
         m_norm = keep.tile([P, 1], F32)
-        denom = keep.tile([P, 1], F32)
-        inv_denom = keep.tile([P, 1], F32)
+        inv_m = keep.tile([P, 1], F32)
+        rho_l_n = keep.tile([P, 1], F32)
+        cross_l_n = keep.tile([P, 1], F32)
+        norm_bias = keep.tile([P, 1], F32)
         rho = keep.tile([P, 1], F32)
         o_sq = keep.tile([P, 1], F32)
         o_norm = keep.tile([P, 1], F32)
@@ -114,16 +113,16 @@ def tile_lowrankredistributor_t_kernel(tc, logits, W, out):
             w0_grouped = ab.tile([P, 2, R, 4], BF16, align_bytes=64)
             wt_grouped = ab.tile([P, V, 2], F32, align_bytes=64)
 
-            nc.sync.dma_start(out=x_sb[:, 0:2, :], in_=x_rows[:, 0:2, :])
-            nc.sync.dma_start(out=x_sb[:, 2:4, :], in_=x_rows[:, 2:4, :])
-            nc.sync.dma_start(out=x_sb[:, 4:8, :], in_=x_rows[:, 4:8, :])
-            nc.sync.dma_start(out=w_raw[:], in_=W.rearrange("(s q e) r -> q s e r", s=4, e=2))
-            for c in range(2, NCHUNK):
-                nc.sync.dma_start(out=x_sb[:, c * CHUNK:(c + 1) * CHUNK, :],
-                                  in_=x_rows[:, c * CHUNK:(c + 1) * CHUNK, :])
+            w_rows = W.rearrange("(s q e) r -> q s e r", s=4, e=2)
+            for s in range(4):
+                nc.sync.dma_start(out=w_raw[:, s], in_=w_rows[:, s])
+            first = 0
+            for n in LOADS:
+                nc.sync.dma_start(out=x_sb[:, first:first + n, :], in_=x_rows[:, first:first + n, :])
+                first += n
 
             gram = bank(7, [P, P], F32, "gram")
-            gram_tiles = [c * CHUNK + i for c in range(NCHUNK) for i in range(GRAM_TILES[c])]
+            gram_tiles = [t for t in range(NT) if SQUARES[t] == "T"]
             xt_bank = {}
 
             def square_on_tensor(t):
@@ -135,7 +134,7 @@ def tile_lowrankredistributor_t_kernel(tc, logits, W, out):
             def square_on_scalar(t, col):
                 squares = ab.tile([P, V], BF16, bufs=2, name="squares")
                 nc.scalar.activation(out=squares[:], in_=x_sb[:, t, :], func=ACT.Square,
-                                     accum_out=sq_scalar[:, col:col + 1])
+                                     accum_out=sq_sums[:, col:col + 1])
 
             def transpose_x(t, index):
                 xt_bank[t] = bank(index, [P, 4, P], F32, "xt_bank")
@@ -152,9 +151,10 @@ def tile_lowrankredistributor_t_kernel(tc, logits, W, out):
                     nc.vector.tensor_copy(out=dst, in_=src)
 
             def regroup_w0(g, u2):
-                nc.vector.tensor_copy(
+                nc.gpsimd.tensor_scalar(
                     out=w0_grouped[:, g, u2 * R2:(u2 + 1) * R2, :].rearrange("q (e p) y -> q e p y", e=2),
-                    in_=w_by_pass[:, g, :, u2 * R2:(u2 + 1) * R2].rearrange("q y (p e) -> q e p y", e=2))
+                    in0=w_by_pass[:, g, :, u2 * R2:(u2 + 1) * R2].rearrange("q y (p e) -> q e p y", e=2),
+                    scalar1=1.0, scalar2=0.0, op0=ALU.mult, op1=ALU.add)
 
             def transpose_w(s, index):
                 wt_bank = bank(index, [P, 2, 2, P], F32, "wt_bank")
@@ -167,46 +167,46 @@ def tile_lowrankredistributor_t_kernel(tc, logits, W, out):
 
             turn = 0
             col = 0
-            for c in range(NCHUNK):
-                tiles = list(range(c * CHUNK, (c + 1) * CHUNK))
-                for t in tiles[GRAM_TILES[c]:]:
-                    square_on_scalar(t, col)
-                    col += 1
-                for t in tiles[:GRAM_TILES[c]]:
-                    square_on_tensor(t)
-                if c < EARLY_CHUNKS:
-                    for t in tiles:
+            first = 0
+            for s in range(4):
+                transpose_w(s, turn % EARLY_BANKS)
+                turn += 1
+            for g in range(2):
+                for u2 in range(2):
+                    regroup_w0(g, u2)
+            for i, n in enumerate(LOADS):
+                tiles = list(range(first, first + n))
+                first += n
+                for t in tiles:
+                    if t < EARLY:
                         transpose_x(t, turn % EARLY_BANKS)
                         turn += 1
                         copy_out_x(t, "vector")
-                if c == 1:
-                    for g in range(2):
-                        for u2 in range(2):
-                            regroup_w0(g, u2)
-                if c == 1 or c == 2:
-                    for s in (2 * c - 2, 2 * c - 1):
-                        transpose_w(s, turn % EARLY_BANKS)
-                        turn += 1
-                if c == 2:
+                for t in tiles:
+                    if SQUARES[t] == "T":
+                        square_on_tensor(t)
+                    else:
+                        square_on_scalar(t, col)
+                        col += 1
+                if i == 5:
                     nc.vector.quantize_mx(out=w0_codes[:].bitcast(FP8X4), scales=w0_scales[:],
                                           in_=w0_grouped[:].rearrange("q g r y -> q (g r y)"))
-                if c == 3:
+                if i == 6:
                     nc.vector.quantize_mx(out=wt_codes[:].bitcast(FP8X4), scales=wt_scales[:],
                                           in_=wt_grouped[:].bitcast(BF16).rearrange("p v y -> p (v y)"))
 
-            late = list(range(EARLY_CHUNKS * CHUNK, NT))
+            late = list(range(EARLY, NT))
             for i, t in enumerate(late[:3]):
                 transpose_x(t, LATE_BANKS[i % 4])
             diagonal = ab.tile([P, P], F32)
             nc.vector.scalar_tensor_tensor(out=diagonal[:], in0=gram[:], scalar=1.0, in1=ident[:],
-                                           op0=ALU.mult, op1=ALU.mult, accum_out=sq_gram[:, 0:1])
+                                           op0=ALU.mult, op1=ALU.mult,
+                                           accum_out=sq_sums[:, SQ_COLS - 1:SQ_COLS])
             copy_out_x(late[0], "vector")
             copy_out_x(late[1], "scalar")
             copy_out_x(late[2], "vector")
-            x2_bank = bank(7, [P, 2 * SQ_COLS], F32, "x2_bank")
-            nc.tensor.matmul(out=x2_bank[:, 0:SQ_COLS], lhsT=ones[:], rhs=sq_gram[:], start=True, stop=True)
-            nc.tensor.matmul(out=x2_bank[:, SQ_COLS:2 * SQ_COLS], lhsT=ones[:], rhs=sq_scalar[:],
-                             start=True, stop=True)
+            x2_bank = bank(7, [P, SQ_COLS], F32, "x2_bank")
+            nc.tensor.matmul(out=x2_bank[:], lhsT=ones[:], rhs=sq_sums[:], start=True, stop=True)
             for i, t in enumerate(late[3:]):
                 transpose_x(t, LATE_BANKS[(i + 3) % 4])
             nc.vector.reduce_sum(out=sum_x2[:], in_=x2_bank[:], axis=AX.X)
@@ -219,7 +219,7 @@ def tile_lowrankredistributor_t_kernel(tc, logits, W, out):
             hg = {}
 
             def new_xs(unit):
-                xs[unit] = ab.tile([P, UNITS[unit][1] * V], BF16, align_bytes=64, bufs=3, name="xs", tag="xs")
+                xs[unit] = ab.tile([P, UNITS[unit][1] * V], BF16, align_bytes=64, bufs=2, name="xs", tag="xs")
 
             def scale_x(unit, engine):
                 t0, nt = UNITS[unit]
@@ -291,27 +291,31 @@ def tile_lowrankredistributor_t_kernel(tc, logits, W, out):
                     quantise_h(i + 1)
                 if VECTOR_SCALED <= i + 5 < NU:
                     scale_x(i + 5, "gpsimd")
+                if i == 0:
+                    nc.vector.tensor_scalar(out=rho_l_n[:], in0=l_n[:], scalar1=(1.0 - ALPHA) / ALPHA, scalar2=None,
+                                            op0=ALU.mult)
+                    nc.vector.tensor_scalar(out=cross_l_n[:], in0=inv_l_n[:], scalar1=cross, scalar2=None, op0=ALU.mult)
+                    nc.vector.tensor_scalar(out=norm_bias[:], in0=inv_l_n[:], scalar1=0.0,
+                                            scalar2=1.0 + ((1.0 - ALPHA) / ALPHA) ** 2, op0=ALU.mult, op1=ALU.add)
                 if i >= 0:
                     sums_of_minted(i)
                 if 0 <= i + 2 < NU:
                     first_matmul(i + 2)
-                for t in waiting[:2]:
+                for t in waiting[:4]:
                     copy_out_x(t, "scalar")
-                waiting = waiting[2:]
+                waiting = waiting[4:]
 
         sums_bank = bank(0, [P, 2, PIECES], F32, "sums_bank")
         nc.tensor.matmul(out=sums_bank[:].rearrange("p a k -> p (a k)"), lhsT=ones[:],
                          rhs=m_sums[:].rearrange("p a k -> p (a k)"), start=True, stop=True)
         nc.vector.reduce_sum(out=totals[:], in_=sums_bank[:], axis=AX.X)
         nc.scalar.activation(out=m_norm[:], in_=totals[:, 0:1], func=ACT.Sqrt)
-        nc.vector.tensor_scalar(out=denom[:], in0=m_norm[:], scalar1=l_n[:, 0:1], scalar2=1.0 / cross,
-                                op0=ALU.mult, op1=ALU.mult)
-        nc.vector.reciprocal(out=inv_denom[:], in_=denom[:])
-        nc.vector.tensor_scalar(out=rho[:], in0=inv_denom[:], scalar1=sum_x2[:, 0:1],
-                                scalar2=(1.0 - ALPHA) / (ALPHA * cross), op0=ALU.mult, op1=ALU.mult)
-        nc.vector.tensor_scalar(out=o_sq[:], in0=totals[:, 1:2], scalar1=inv_denom[:, 0:1],
-                                scalar2=ALPHA * ALPHA + (1.0 - ALPHA) * (1.0 - ALPHA), op0=ALU.mult, op1=ALU.add)
-        nc.scalar.activation(out=o_norm[:], in_=o_sq[:], func=ACT.Sqrt, scale=1.0 / (ALPHA * ALPHA))
+        nc.vector.reciprocal(out=inv_m[:], in_=m_norm[:])
+        nc.vector.tensor_scalar(out=rho[:], in0=inv_m[:], scalar1=rho_l_n[:, 0:1], scalar2=None, op0=ALU.mult)
+        nc.vector.scalar_tensor_tensor(out=o_sq[:], in0=totals[:, 1:2], scalar=inv_m[:, 0:1], in1=cross_l_n[:],
+                                       op0=ALU.mult, op1=ALU.mult)
+        nc.scalar.activation(out=o_norm[:], in_=o_sq[:], func=ACT.Sqrt, bias=norm_bias[:, 0:1],
+                             scale=1.0 / (ALPHA * ALPHA))
 
         with tc.tile_pool(name="cc", bufs=1) as cc:
             first = 0

@@ -37,7 +37,7 @@ VECTOR_SCALED = 6
 H_BANKS = [0, 1, 2]
 M_BANKS = [7, 3, 4, 5, 6]
 
-STORE_PIECES = [1, 1, 2] + [4] * 14 + [2, 1, 1]
+STORES = ["A", "B", "A", "A", "AB", "AA"] + ["AAAB"] * 13 + ["AA", "AA"]
 
 
 def tile_lowrankredistributor_t_kernel(tc, logits, W, out):
@@ -319,23 +319,13 @@ def tile_lowrankredistributor_t_kernel(tc, logits, W, out):
 
         with tc.tile_pool(name="cc", bufs=1) as cc:
             first = 0
-            fours = 0
-            for n_pieces in STORE_PIECES:
-                stage = cc.tile([P, n_pieces * BANK], F32, bufs=6, name="stage", tag="stage")
-                other_way = 0
-                beta_on_gpsimd = 0
-                if n_pieces == 4:
-                    if fours % 3 < 2:
-                        other_way = 1
-                    else:
-                        beta_on_gpsimd = 2
-                    fours += 1
-                on_vector = n_pieces - other_way
-                for i in range(n_pieces):
+            for ways in STORES:
+                stage = cc.tile([P, len(ways) * BANK], F32, bufs=9, name="stage", tag="stage")
+                for i, way in enumerate(ways):
                     piece = first + i
                     cols = slice(i * BANK, (i + 1) * BANK)
                     minted = second_matmul(piece, (piece + 1) % 8)
-                    if i < on_vector:
+                    if way != "B":
                         nc.vector.scalar_tensor_tensor(out=stage[:, cols], in0=minted[:], scalar=rho[:, 0:1],
                                                        in1=x_piece(piece), op0=ALU.mult, op1=ALU.add)
                         if piece == 0:
@@ -350,12 +340,9 @@ def tile_lowrankredistributor_t_kernel(tc, logits, W, out):
                                              scale=rho_beta[:, 0:1])
                         nc.gpsimd.tensor_tensor(out=stage[:, cols], in0=stage[:, cols], in1=beta_logits[:],
                                                 op=ALU.add)
-                on_scalar = slice(0, (on_vector - beta_on_gpsimd) * BANK)
-                nc.scalar.activation(out=stage[:, on_scalar], in_=stage[:, on_scalar], func=ACT.Copy,
-                                     scale=beta[:, 0:1])
-                if beta_on_gpsimd:
-                    rest = slice((on_vector - beta_on_gpsimd) * BANK, on_vector * BANK)
-                    nc.gpsimd.tensor_scalar(out=stage[:, rest], in0=stage[:, rest], scalar1=beta[:, 0:1],
-                                            scalar2=0.0, op0=ALU.mult, op1=ALU.add)
-                nc.sync.dma_start(out=out_rows[:, first * BANK:(first + n_pieces) * BANK], in_=stage[:])
-                first += n_pieces
+                if "A" in ways:
+                    on_scalar = slice(0, ways.count("A") * BANK)
+                    nc.scalar.activation(out=stage[:, on_scalar], in_=stage[:, on_scalar], func=ACT.Copy,
+                                         scale=beta[:, 0:1])
+                nc.sync.dma_start(out=out_rows[:, first * BANK:(first + len(ways)) * BANK], in_=stage[:])
+                first += len(ways)

@@ -56,6 +56,8 @@ def tile_lowrankredistributor_t_kernel(tc, logits, W, out):
         warm = keep.tile([P, 1], F32)
         nc.vector.memset(warm[:], 1.0)
         nc.scalar.activation(out=warm[:], in_=warm[:], func=ACT.Sqrt)
+        warm_sb = keep.tile([P, BANK], BF16)
+        nc.vector.memset(warm_sb[:], 1.0)
         ident = keep.tile([P, P], F32)
         make_identity(nc, ident[:])
         ones = keep.tile([P, P], F32)
@@ -121,6 +123,12 @@ def tile_lowrankredistributor_t_kernel(tc, logits, W, out):
                 nc.sync.dma_start(out=x_sb[:, first:first + n, :], in_=x_rows[:, first:first + n, :])
                 first += n
 
+            def keep_warm(n):
+                for i in range(n):
+                    idle = bank(2, [P, BANK], F32, "idle")
+                    nc.tensor.matmul(out=idle[:], lhsT=warm_sb[:, 0:P], rhs=warm_sb[:], start=True, stop=True)
+
+            keep_warm(6)
             gram = bank(7, [P, P], F32, "gram")
             gram_tiles = [t for t in range(NT) if SQUARES[t] == "T"]
             xt_bank = {}
@@ -198,6 +206,7 @@ def tile_lowrankredistributor_t_kernel(tc, logits, W, out):
             late = list(range(EARLY, NT))
             for i, t in enumerate(late[:3]):
                 transpose_x(t, LATE_BANKS[i % 4])
+            keep_warm(2)
             diagonal = ab.tile([P, P], F32)
             nc.vector.scalar_tensor_tensor(out=diagonal[:], in0=gram[:], scalar=1.0, in1=ident[:],
                                            op0=ALU.mult, op1=ALU.mult,
@@ -209,6 +218,8 @@ def tile_lowrankredistributor_t_kernel(tc, logits, W, out):
             nc.tensor.matmul(out=x2_bank[:], lhsT=ones[:], rhs=sq_sums[:], start=True, stop=True)
             for i, t in enumerate(late[3:]):
                 transpose_x(t, LATE_BANKS[(i + 3) % 4])
+                if i % 2 == 1:
+                    keep_warm(1)
             nc.vector.reduce_sum(out=sum_x2[:], in_=x2_bank[:], axis=AX.X)
             nc.scalar.activation(out=l_n[:], in_=sum_x2[:], func=ACT.Sqrt)
             nc.vector.reciprocal(out=inv_l_n[:], in_=l_n[:])

@@ -37,7 +37,7 @@ VECTOR_SCALED = 6
 H_BANKS = [0, 1, 2]
 M_BANKS = [7, 3, 4, 5, 6]
 
-STORES = ["A", "B", "A", "A", "AB", "AA"] + ["AAAB"] * 13 + ["AA", "AA"]
+STORES = ["A", "B", "A", "A", "AB", "AA"] + ["AAAB", "AAAB", "AACC"] * 4 + ["AAAB", "AA", "AA"]
 
 
 def tile_lowrankredistributor_t_kernel(tc, logits, W, out):
@@ -128,7 +128,7 @@ def tile_lowrankredistributor_t_kernel(tc, logits, W, out):
                     idle = bank(2, [P, BANK], F32, "idle")
                     nc.tensor.matmul(out=idle[:], lhsT=warm_sb[:, 0:P], rhs=warm_sb[:], start=True, stop=True)
 
-            keep_warm(6)
+            keep_warm(3)
             gram = bank(7, [P, P], F32, "gram")
             gram_tiles = [t for t in range(NT) if SQUARES[t] == "T"]
             xt_bank = {}
@@ -355,5 +355,9 @@ def tile_lowrankredistributor_t_kernel(tc, logits, W, out):
                     on_scalar = slice(0, ways.count("A") * BANK)
                     nc.scalar.activation(out=stage[:, on_scalar], in_=stage[:, on_scalar], func=ACT.Copy,
                                          scale=beta[:, 0:1])
+                if "C" in ways:
+                    on_gpsimd = slice(ways.index("C") * BANK, (ways.index("C") + ways.count("C")) * BANK)
+                    nc.gpsimd.tensor_scalar(out=stage[:, on_gpsimd], in0=stage[:, on_gpsimd], scalar1=beta[:, 0:1],
+                                            scalar2=0.0, op0=ALU.mult, op1=ALU.add)
                 nc.sync.dma_start(out=out_rows[:, first * BANK:(first + len(ways)) * BANK], in_=stage[:])
                 first += len(ways)

@@ -33,7 +33,7 @@ LATE_BANKS = [3, 4, 5, 6]
 
 UNITS = [(0, 1), (1, 1)] + [(t, 2) for t in range(2, NT, 2)]
 NU = len(UNITS)
-VECTOR_SCALED = 6
+VECTOR_SCALED = 17
 H_BANKS = [0, 1, 2]
 M_BANKS = [7, 3, 4, 5, 6]
 
@@ -56,8 +56,6 @@ def tile_lowrankredistributor_t_kernel(tc, logits, W, out):
         warm = keep.tile([P, 1], F32)
         nc.vector.memset(warm[:], 1.0)
         nc.scalar.activation(out=warm[:], in_=warm[:], func=ACT.Sqrt)
-        warm_sb = keep.tile([P, BANK], BF16)
-        nc.vector.memset(warm_sb[:], 1.0)
         ident = keep.tile([P, P], F32)
         make_identity(nc, ident[:])
         ones = keep.tile([P, P], F32)
@@ -73,7 +71,7 @@ def tile_lowrankredistributor_t_kernel(tc, logits, W, out):
         h_scales = keep.tile([P, B], U8, align_bytes=64)
         sq_sums = keep.tile([P, SQ_COLS], F32)
         nc.vector.memset(sq_sums[:], 0.0)
-        m_sums = keep.tile([P, 2, PIECES], F32)
+        m_sums = keep.tile([P, PIECES, 2], F32)
         sum_x2 = keep.tile([P, 1], F32)
         l_n = keep.tile([P, 1], F32)
         inv_l_n = keep.tile([P, 1], F32)
@@ -123,12 +121,6 @@ def tile_lowrankredistributor_t_kernel(tc, logits, W, out):
                 nc.sync.dma_start(out=x_sb[:, first:first + n, :], in_=x_rows[:, first:first + n, :])
                 first += n
 
-            def keep_warm(n):
-                for i in range(n):
-                    idle = bank(2, [P, BANK], F32, "idle")
-                    nc.tensor.matmul(out=idle[:], lhsT=warm_sb[:, 0:P], rhs=warm_sb[:], start=True, stop=True)
-
-            keep_warm(3)
             gram = bank(7, [P, P], F32, "gram")
             gram_tiles = [t for t in range(NT) if SQUARES[t] == "T"]
             xt_bank = {}
@@ -206,7 +198,6 @@ def tile_lowrankredistributor_t_kernel(tc, logits, W, out):
             late = list(range(EARLY, NT))
             for i, t in enumerate(late[:3]):
                 transpose_x(t, LATE_BANKS[i % 4])
-            keep_warm(2)
             diagonal = ab.tile([P, P], F32)
             nc.vector.scalar_tensor_tensor(out=diagonal[:], in0=gram[:], scalar=1.0, in1=ident[:],
                                            op0=ALU.mult, op1=ALU.mult,
@@ -218,8 +209,6 @@ def tile_lowrankredistributor_t_kernel(tc, logits, W, out):
             nc.tensor.matmul(out=x2_bank[:], lhsT=ones[:], rhs=sq_sums[:], start=True, stop=True)
             for i, t in enumerate(late[3:]):
                 transpose_x(t, LATE_BANKS[(i + 3) % 4])
-                if i % 2 == 1:
-                    keep_warm(1)
             nc.vector.reduce_sum(out=sum_x2[:], in_=x2_bank[:], axis=AX.X)
             nc.scalar.activation(out=l_n[:], in_=sum_x2[:], func=ACT.Sqrt)
             nc.vector.reciprocal(out=inv_l_n[:], in_=l_n[:])
@@ -280,11 +269,11 @@ def tile_lowrankredistributor_t_kernel(tc, logits, W, out):
                     minted = second_matmul(piece, M_BANKS[piece % 5])
                     squares_m = ab.tile([P, BANK], BF16, bufs=2, name="squares_m")
                     nc.scalar.activation(out=squares_m[:], in_=minted[:], func=ACT.Square,
-                                         accum_out=m_sums[:, 0, piece:piece + 1])
+                                         accum_out=m_sums[:, piece, 0:1])
                     products = ab.tile([P, BANK], F32, bufs=2, name="products")
                     nc.vector.scalar_tensor_tensor(out=products[:], in0=minted[:], scalar=1.0, in1=x_piece(piece),
                                                    op0=ALU.mult, op1=ALU.mult,
-                                                   accum_out=m_sums[:, 1, piece:piece + 1])
+                                                   accum_out=m_sums[:, piece, 1:2])
 
             new_xs(0)
             scale_x(0, "vector")
@@ -316,10 +305,11 @@ def tile_lowrankredistributor_t_kernel(tc, logits, W, out):
                     copy_out_x(t, "scalar")
                 waiting = waiting[4:]
 
-        sums_bank = bank(0, [P, 2, PIECES], F32, "sums_bank")
-        nc.tensor.matmul(out=sums_bank[:].rearrange("p a k -> p (a k)"), lhsT=ones[:],
-                         rhs=m_sums[:].rearrange("p a k -> p (a k)"), start=True, stop=True)
-        nc.vector.reduce_sum(out=totals[:], in_=sums_bank[:], axis=AX.X)
+        sums_bank = bank(0, [P, PIECES, 2], F32, "sums_bank")
+        for pieces in (slice(0, 2 * UNITS[-1][0]), slice(2 * UNITS[-1][0], PIECES)):
+            nc.tensor.matmul(out=sums_bank[:, pieces].rearrange("p k a -> p (k a)"), lhsT=ones[:],
+                             rhs=m_sums[:, pieces].rearrange("p k a -> p (k a)"), start=True, stop=True)
+        nc.vector.reduce_sum(out=totals[:], in_=sums_bank[:].rearrange("p k a -> p a k"), axis=AX.X)
         nc.scalar.activation(out=m_norm[:], in_=totals[:, 0:1], func=ACT.Sqrt)
         nc.vector.reciprocal(out=inv_m[:], in_=m_norm[:])
         nc.vector.tensor_scalar(out=rho[:], in0=inv_m[:], scalar1=rho_l_n[:, 0:1], scalar2=None, op0=ALU.mult)

@@ -31,9 +31,9 @@ EARLY = 24
 EARLY_BANKS = 7
 LATE_BANKS = [3, 4, 5, 6]
 
-UNITS = [(0, 1), (1, 1)] + [(t, 2) for t in range(2, NT, 2)]
+UNITS = [(0, 1)] + [(t, 2) for t in range(1, NT - 1, 2)] + [(NT - 1, 1)]
 NU = len(UNITS)
-VECTOR_SCALED = 17
+VECTOR_SCALED = 6
 H_BANKS = [0, 1, 2]
 M_BANKS = [7, 3, 4, 5, 6]
 
@@ -71,12 +71,16 @@ def tile_lowrankredistributor_t_kernel(tc, logits, W, out):
         h_scales = keep.tile([P, B], U8, align_bytes=64)
         sq_sums = keep.tile([P, SQ_COLS], F32)
         nc.vector.memset(sq_sums[:], 0.0)
-        m_sums = keep.tile([P, PIECES, 2], F32)
+        m_sq_sums = keep.tile([P, PIECES], F32)
+        m_x_sums = keep.tile([P, PIECES], F32)
+        x2_copy = keep.tile([P, SQ_COLS], F32)
         sum_x2 = keep.tile([P, 1], F32)
         l_n = keep.tile([P, 1], F32)
         inv_l_n = keep.tile([P, 1], F32)
         inv_l_n_gp = keep.tile([P, 1], F32)
-        totals = keep.tile([P, 2], F32)
+        m_copy = keep.tile([P, PIECES], F32)
+        m_sq = keep.tile([P, 1], F32)
+        m_x = keep.tile([P, 1], F32)
         m_norm = keep.tile([P, 1], F32)
         inv_m = keep.tile([P, 1], F32)
         rho_l_n = keep.tile([P, 1], F32)
@@ -209,7 +213,7 @@ def tile_lowrankredistributor_t_kernel(tc, logits, W, out):
             nc.tensor.matmul(out=x2_bank[:], lhsT=ones[:], rhs=sq_sums[:], start=True, stop=True)
             for i, t in enumerate(late[3:]):
                 transpose_x(t, LATE_BANKS[(i + 3) % 4])
-            nc.vector.reduce_sum(out=sum_x2[:], in_=x2_bank[:], axis=AX.X)
+            nc.scalar.activation(out=x2_copy[:], in_=x2_bank[:], func=ACT.Copy, accum_out=sum_x2[:])
             nc.scalar.activation(out=l_n[:], in_=sum_x2[:], func=ACT.Sqrt)
             nc.vector.reciprocal(out=inv_l_n[:], in_=l_n[:])
             waiting = late[3:]
@@ -269,11 +273,11 @@ def tile_lowrankredistributor_t_kernel(tc, logits, W, out):
                     minted = second_matmul(piece, M_BANKS[piece % 5])
                     squares_m = ab.tile([P, BANK], BF16, bufs=2, name="squares_m")
                     nc.scalar.activation(out=squares_m[:], in_=minted[:], func=ACT.Square,
-                                         accum_out=m_sums[:, piece, 0:1])
+                                         accum_out=m_sq_sums[:, piece:piece + 1])
                     products = ab.tile([P, BANK], F32, bufs=2, name="products")
                     nc.vector.scalar_tensor_tensor(out=products[:], in0=minted[:], scalar=1.0, in1=x_piece(piece),
                                                    op0=ALU.mult, op1=ALU.mult,
-                                                   accum_out=m_sums[:, piece, 1:2])
+                                                   accum_out=m_x_sums[:, piece:piece + 1])
 
             new_xs(0)
             scale_x(0, "vector")
@@ -305,15 +309,18 @@ def tile_lowrankredistributor_t_kernel(tc, logits, W, out):
                     copy_out_x(t, "scalar")
                 waiting = waiting[4:]
 
-        sums_bank = bank(0, [P, PIECES, 2], F32, "sums_bank")
-        for pieces in (slice(0, 2 * UNITS[-1][0]), slice(2 * UNITS[-1][0], PIECES)):
-            nc.tensor.matmul(out=sums_bank[:, pieces].rearrange("p k a -> p (k a)"), lhsT=ones[:],
-                             rhs=m_sums[:, pieces].rearrange("p k a -> p (k a)"), start=True, stop=True)
-        nc.vector.reduce_sum(out=totals[:], in_=sums_bank[:].rearrange("p k a -> p a k"), axis=AX.X)
-        nc.scalar.activation(out=m_norm[:], in_=totals[:, 0:1], func=ACT.Sqrt)
+        m_sq_bank = bank(0, [P, PIECES], F32, "m_sq_bank")
+        m_x_bank = bank(1, [P, PIECES], F32, "m_x_bank")
+        last = 2 * UNITS[-1][0]
+        for pieces in (slice(0, last), slice(last, PIECES)):
+            for sums_bank, sums in ((m_sq_bank, m_sq_sums), (m_x_bank, m_x_sums)):
+                nc.tensor.matmul(out=sums_bank[:, pieces], lhsT=ones[:], rhs=sums[:, pieces], start=True, stop=True)
+        nc.scalar.activation(out=m_copy[:], in_=m_sq_bank[:], func=ACT.Copy, accum_out=m_sq[:])
+        nc.scalar.activation(out=m_norm[:], in_=m_sq[:], func=ACT.Sqrt)
         nc.vector.reciprocal(out=inv_m[:], in_=m_norm[:])
         nc.vector.tensor_scalar(out=rho[:], in0=inv_m[:], scalar1=rho_l_n[:, 0:1], scalar2=None, op0=ALU.mult)
-        nc.vector.scalar_tensor_tensor(out=o_sq[:], in0=totals[:, 1:2], scalar=inv_m[:, 0:1], in1=cross_l_n[:],
+        nc.vector.reduce_sum(out=m_x[:], in_=m_x_bank[:], axis=AX.X)
+        nc.vector.scalar_tensor_tensor(out=o_sq[:], in0=m_x[:], scalar=inv_m[:, 0:1], in1=cross_l_n[:],
                                        op0=ALU.mult, op1=ALU.mult)
         nc.scalar.activation(out=o_norm[:], in_=o_sq[:], func=ACT.Sqrt, bias=norm_bias[:, 0:1],
                              scale=1.0 / (ALPHA * ALPHA))
@@ -325,7 +332,7 @@ def tile_lowrankredistributor_t_kernel(tc, logits, W, out):
                 for i, way in enumerate(ways):
                     piece = first + i
                     cols = slice(i * BANK, (i + 1) * BANK)
-                    minted = second_matmul(piece, (piece + 1) % 8)
+                    minted = second_matmul(piece, (piece + 2) % 8)
                     if way != "B":
                         nc.vector.scalar_tensor_tensor(out=stage[:, cols], in0=minted[:], scalar=rho[:, 0:1],
                                                        in1=x_piece(piece), op0=ALU.mult, op1=ALU.add)

@@ -37,7 +37,8 @@ VECTOR_SCALED = 6
 H_BANKS = [0, 1, 2]
 M_BANKS = [7, 3, 4, 5, 6]
 
-STORES = ["A", "B", "A", "A", "AB", "AA"] + ["AAAB", "AAAB", "AACC"] * 4 + ["AAAB", "AA", "AA"]
+STORES = (["A", "B", "A", "A", "AB", "AA", "AAAB", "AAAB", "AACC", "AAAB"]
+          + ["AAAB AACC", "AAAB AAAB", "AACC AAAB", "AAAB AACC"] + ["AAAB", "AAAA"])
 
 
 def tile_lowrankredistributor_t_kernel(tc, logits, W, out):
@@ -60,6 +61,9 @@ def tile_lowrankredistributor_t_kernel(tc, logits, W, out):
         make_identity(nc, ident[:])
         ones = keep.tile([P, P], F32)
         nc.vector.memset(ones[:], 1.0)
+        norm_bias = keep.tile([P, 1], F32)
+        nc.vector.tensor_scalar(out=norm_bias[:], in0=ones[:, 0:1], scalar1=0.0,
+                                scalar2=1.0 + ((1.0 - ALPHA) / ALPHA) ** 2, op0=ALU.mult, op1=ALU.add)
 
         x_sb = keep.tile([P, NT, V], BF16)
         x_words = x_sb[:].bitcast(F32)
@@ -85,7 +89,6 @@ def tile_lowrankredistributor_t_kernel(tc, logits, W, out):
         inv_m = keep.tile([P, 1], F32)
         rho_l_n = keep.tile([P, 1], F32)
         cross_l_n = keep.tile([P, 1], F32)
-        norm_bias = keep.tile([P, 1], F32)
         rho = keep.tile([P, 1], F32)
         o_sq = keep.tile([P, 1], F32)
         o_norm = keep.tile([P, 1], F32)
@@ -135,9 +138,9 @@ def tile_lowrankredistributor_t_kernel(tc, logits, W, out):
                     nc.tensor.matmul(out=gram[:], lhsT=block, rhs=block, start=(t == gram_tiles[0] and j == 0),
                                      stop=(t == gram_tiles[-1] and j == V // P - 1))
 
-            def square_on_scalar(t, col):
-                squares = ab.tile([P, V], BF16, bufs=2, name="squares")
-                nc.scalar.activation(out=squares[:], in_=x_sb[:, t, :], func=ACT.Square,
+            def square_on_scalar(t, n, col):
+                squares = ab.tile([P, 2, V], BF16, bufs=2, name="squares")
+                nc.scalar.activation(out=squares[:, 0:n, :], in_=x_sb[:, t:t + n, :], func=ACT.Square,
                                      accum_out=sq_sums[:, col:col + 1])
 
             def transpose_x(t, index):
@@ -189,9 +192,10 @@ def tile_lowrankredistributor_t_kernel(tc, logits, W, out):
                 for t in tiles:
                     if SQUARES[t] == "T":
                         square_on_tensor(t)
-                    else:
-                        square_on_scalar(t, col)
-                        col += 1
+                on_scalar = [t for t in tiles if SQUARES[t] == "S"]
+                if on_scalar:
+                    square_on_scalar(on_scalar[0], len(on_scalar), col)
+                    col += 1
                 if i == 5:
                     nc.vector.quantize_mx(out=w0_codes[:].bitcast(FP8X4), scales=w0_scales[:],
                                           in_=w0_grouped[:].rearrange("q g r y -> q (g r y)"))
@@ -225,14 +229,16 @@ def tile_lowrankredistributor_t_kernel(tc, logits, W, out):
             def new_xs(unit):
                 xs[unit] = ab.tile([P, UNITS[unit][1] * V], BF16, align_bytes=64, bufs=2, name="xs", tag="xs")
 
-            def scale_x(unit, engine):
+            def scale_x(unit, engine, lo=0, hi=2):
                 t0, nt = UNITS[unit]
-                src = xt[:, t0:t0 + nt, :].rearrange("q t v -> q (t v)")
+                hi = min(hi, nt)
+                src = xt[:, t0 + lo:t0 + hi, :].rearrange("q t v -> q (t v)")
+                dst = xs[unit][:, lo * V:hi * V]
                 if engine == "gpsimd":
-                    nc.gpsimd.tensor_scalar(out=xs[unit][:], in0=src, scalar1=inv_l_n_gp[:, 0:1], scalar2=0.0,
+                    nc.gpsimd.tensor_scalar(out=dst, in0=src, scalar1=inv_l_n_gp[:, 0:1], scalar2=0.0,
                                             op0=ALU.mult, op1=ALU.add)
                 else:
-                    nc.vector.tensor_scalar(out=xs[unit][:], in0=src, scalar1=inv_l_n[:, 0:1], scalar2=None,
+                    nc.vector.tensor_scalar(out=dst, in0=src, scalar1=inv_l_n[:, 0:1], scalar2=None,
                                             op0=ALU.mult)
 
             def quantise_x(unit):
@@ -281,13 +287,17 @@ def tile_lowrankredistributor_t_kernel(tc, logits, W, out):
 
             new_xs(0)
             scale_x(0, "vector")
+            new_xs(1)
+            scale_x(1, "vector", 0, 1)
+            quantise_x(0)
+            scale_x(1, "vector", 1, 2)
             for i in range(-3, NU):
-                if i + 4 < VECTOR_SCALED:
+                if 2 <= i + 4 < VECTOR_SCALED:
                     new_xs(i + 4)
                     scale_x(i + 4, "vector")
                 if VECTOR_SCALED <= i + 5 < NU:
                     new_xs(i + 5)
-                if i + 3 < NU:
+                if 1 <= i + 3 < NU:
                     quantise_x(i + 3)
                 if i + 5 == VECTOR_SCALED:
                     nc.vector.tensor_copy(out=inv_l_n_gp[:], in_=inv_l_n[:])
@@ -295,12 +305,11 @@ def tile_lowrankredistributor_t_kernel(tc, logits, W, out):
                     quantise_h(i + 1)
                 if VECTOR_SCALED <= i + 5 < NU:
                     scale_x(i + 5, "gpsimd")
-                if i == 0:
-                    nc.vector.tensor_scalar(out=rho_l_n[:], in0=l_n[:], scalar1=(1.0 - ALPHA) / ALPHA, scalar2=None,
-                                            op0=ALU.mult)
-                    nc.vector.tensor_scalar(out=cross_l_n[:], in0=inv_l_n[:], scalar1=cross, scalar2=None, op0=ALU.mult)
-                    nc.vector.tensor_scalar(out=norm_bias[:], in0=inv_l_n[:], scalar1=0.0,
-                                            scalar2=1.0 + ((1.0 - ALPHA) / ALPHA) ** 2, op0=ALU.mult, op1=ALU.add)
+                if i + 5 == VECTOR_SCALED:
+                    nc.gpsimd.tensor_scalar(out=rho_l_n[:], in0=l_n[:], scalar1=(1.0 - ALPHA) / ALPHA, scalar2=0.0,
+                                            op0=ALU.mult, op1=ALU.add)
+                    nc.gpsimd.tensor_scalar(out=cross_l_n[:], in0=inv_l_n[:], scalar1=cross, scalar2=0.0,
+                                            op0=ALU.mult, op1=ALU.add)
                 if i >= 0:
                     sums_of_minted(i)
                 if 0 <= i + 2 < NU:
@@ -327,34 +336,40 @@ def tile_lowrankredistributor_t_kernel(tc, logits, W, out):
 
         with tc.tile_pool(name="cc", bufs=1) as cc:
             first = 0
-            for ways in STORES:
-                stage = cc.tile([P, len(ways) * BANK], F32, bufs=9, name="stage", tag="stage")
-                for i, way in enumerate(ways):
-                    piece = first + i
-                    cols = slice(i * BANK, (i + 1) * BANK)
-                    minted = second_matmul(piece, (piece + 2) % 8)
-                    if way != "B":
-                        nc.vector.scalar_tensor_tensor(out=stage[:, cols], in0=minted[:], scalar=rho[:, 0:1],
-                                                       in1=x_piece(piece), op0=ALU.mult, op1=ALU.add)
-                        if piece == 0:
-                            nc.vector.reciprocal(out=beta[:], in_=o_norm[:])
-                            nc.vector.tensor_scalar(out=rho_beta[:], in0=rho[:], scalar1=beta[:, 0:1], scalar2=None,
-                                                    op0=ALU.mult)
-                    else:
-                        beta_logits = cc.tile([P, BANK], F32, bufs=3, name="beta_logits", tag="beta_logits")
-                        nc.gpsimd.tensor_scalar(out=beta_logits[:], in0=x_piece(piece), scalar1=beta[:, 0:1],
+            for groups in STORES:
+                n_pieces = len(groups.replace(" ", ""))
+                stage = cc.tile([P, n_pieces * BANK], F32, bufs=7, name="stage", tag="stage")
+                start = 0
+                for ways in groups.split(" "):
+                    for i, way in enumerate(ways):
+                        piece = first + start + i
+                        cols = slice((start + i) * BANK, (start + i + 1) * BANK)
+                        minted = second_matmul(piece, (piece + 2) % 8)
+                        if way != "B":
+                            nc.vector.scalar_tensor_tensor(out=stage[:, cols], in0=minted[:], scalar=rho[:, 0:1],
+                                                           in1=x_piece(piece), op0=ALU.mult, op1=ALU.add)
+                            if piece == 0:
+                                nc.vector.reciprocal(out=beta[:], in_=o_norm[:])
+                                nc.vector.tensor_scalar(out=rho_beta[:], in0=rho[:], scalar1=beta[:, 0:1], scalar2=None,
+                                                        op0=ALU.mult)
+                                nc.vector.tensor_scalar(out=stage[:, cols], in0=stage[:, cols], scalar1=beta[:, 0:1],
+                                                        scalar2=None, op0=ALU.mult)
+                        else:
+                            beta_logits = cc.tile([P, BANK], F32, bufs=3, name="beta_logits", tag="beta_logits")
+                            nc.gpsimd.tensor_scalar(out=beta_logits[:], in0=x_piece(piece), scalar1=beta[:, 0:1],
+                                                    scalar2=0.0, op0=ALU.mult, op1=ALU.add)
+                            nc.scalar.activation(out=stage[:, cols], in_=minted[:], func=ACT.Copy,
+                                                 scale=rho_beta[:, 0:1])
+                            nc.gpsimd.tensor_tensor(out=stage[:, cols], in0=stage[:, cols], in1=beta_logits[:],
+                                                    op=ALU.add)
+                    if "A" in ways and first + start > 0:
+                        on_scalar = slice(start * BANK, (start + ways.count("A")) * BANK)
+                        nc.scalar.activation(out=stage[:, on_scalar], in_=stage[:, on_scalar], func=ACT.Copy,
+                                             scale=beta[:, 0:1])
+                    if "C" in ways:
+                        on_gpsimd = slice((start + ways.index("C")) * BANK, (start + len(ways)) * BANK)
+                        nc.gpsimd.tensor_scalar(out=stage[:, on_gpsimd], in0=stage[:, on_gpsimd], scalar1=beta[:, 0:1],
                                                 scalar2=0.0, op0=ALU.mult, op1=ALU.add)
-                        nc.scalar.activation(out=stage[:, cols], in_=minted[:], func=ACT.Copy,
-                                             scale=rho_beta[:, 0:1])
-                        nc.gpsimd.tensor_tensor(out=stage[:, cols], in0=stage[:, cols], in1=beta_logits[:],
-                                                op=ALU.add)
-                if "A" in ways:
-                    on_scalar = slice(0, ways.count("A") * BANK)
-                    nc.scalar.activation(out=stage[:, on_scalar], in_=stage[:, on_scalar], func=ACT.Copy,
-                                         scale=beta[:, 0:1])
-                if "C" in ways:
-                    on_gpsimd = slice(ways.index("C") * BANK, (ways.index("C") + ways.count("C")) * BANK)
-                    nc.gpsimd.tensor_scalar(out=stage[:, on_gpsimd], in0=stage[:, on_gpsimd], scalar1=beta[:, 0:1],
-                                            scalar2=0.0, op0=ALU.mult, op1=ALU.add)
-                nc.sync.dma_start(out=out_rows[:, first * BANK:(first + len(ways)) * BANK], in_=stage[:])
-                first += len(ways)
+                    start += len(ways)
+                nc.sync.dma_start(out=out_rows[:, first * BANK:(first + n_pieces) * BANK], in_=stage[:])
+                first += n_pieces

@@ -34,8 +34,8 @@ LATE_BANKS = [3, 4, 5, 6]
 UNITS = [(0, 1)] + [(t, 2) for t in range(1, NT - 1, 2)] + [(NT - 1, 1)]
 NU = len(UNITS)
 VECTOR_SCALED = 6
-H_BANKS = [0, 1, 2]
-M_BANKS = [7, 3, 4, 5, 6]
+H_BANKS = [0, 1]
+M_BANKS = [7, 2, 3, 4, 5, 6]
 
 STORES = (["A", "B", "A", "A", "AB", "AA", "AAAB", "AAAB", "AACC", "AAAB"]
           + ["AAAB AACC", "AAAB AAAB", "AACC AAAB", "AAAB AACC"] + ["AAAB", "AAAA"])
@@ -253,7 +253,7 @@ def tile_lowrankredistributor_t_kernel(tc, logits, W, out):
                 codes, scales = xq[unit]
                 hg[unit] = ab.tile([P, nt, P, 4], BF16, align_bytes=64, bufs=3, name="hg", tag="hg")
                 for i in range(nt):
-                    h_bank = bank(H_BANKS[(t0 + i) % 3], [P, 4, P], F32, "h_bank")
+                    h_bank = bank(H_BANKS[(t0 + i) % 2], [P, 4, P], F32, "h_bank")
                     for y in range(4):
                         for g in range(2):
                             w_cols = slice(g * R + y * P, g * R + (y + 1) * P)
@@ -273,10 +273,10 @@ def tile_lowrankredistributor_t_kernel(tc, logits, W, out):
                                       scales=h_scales[:, t0 * P:(t0 + nt) * P],
                                       in_=hg[unit][:].rearrange("p t n y -> p (t n y)"))
 
-            def sums_of_minted(unit):
+            def sums_of_minted(unit, pieces):
                 t0, nt = UNITS[unit]
-                for piece in range(2 * t0, 2 * (t0 + nt)):
-                    minted = second_matmul(piece, M_BANKS[piece % 5])
+                for piece in range(2 * t0, 2 * (t0 + nt))[pieces]:
+                    minted = second_matmul(piece, M_BANKS[piece % 6])
                     squares_m = ab.tile([P, BANK], BF16, bufs=2, name="squares_m")
                     nc.scalar.activation(out=squares_m[:], in_=minted[:], func=ACT.Square,
                                          accum_out=m_sq_sums[:, piece:piece + 1])
@@ -311,9 +311,11 @@ def tile_lowrankredistributor_t_kernel(tc, logits, W, out):
                     nc.gpsimd.tensor_scalar(out=cross_l_n[:], in0=inv_l_n[:], scalar1=cross, scalar2=0.0,
                                             op0=ALU.mult, op1=ALU.add)
                 if i >= 0:
-                    sums_of_minted(i)
+                    sums_of_minted(i, slice(0, 3))
                 if 0 <= i + 2 < NU:
                     first_matmul(i + 2)
+                if i >= 0:
+                    sums_of_minted(i, slice(3, None))
                 for t in waiting[:4]:
                     copy_out_x(t, "scalar")
                 waiting = waiting[4:]

from contextlib import ExitStack

import concourse.mybir as mybir
from concourse.masks import make_identity

FP8X4 = mybir.dt.float8_e4m3fn_x4
BF16 = mybir.dt.bfloat16
F32 = mybir.dt.float32
U32 = mybir.dt.uint32
U8 = mybir.dt.uint8
ALU = mybir.AluOpType
ACT = mybir.ActivationFunctionType
AX = mybir.AxisListType

P = 128
B, V, R = 4096, 1024, 512
ALPHA = 0.3
FLOPS = 2 * B * V * R * 2

NT = B // P
BANK = 512
PIECES = NT * V // BANK
TILE_WORDS = V // 4
SLAB = V // 4
R2 = R // 2

LOADS = [1, 1, 2, 4, 4, 4, 4, 4, 4, 2, 1, 1]
SQUARES = "TTSS" * 8
SQ_COLS = 32
EARLY = 24
EARLY_BANKS = 7
LATE_BANKS = [3, 4, 5, 6]

UNITS = [(0, 1)] + [(t, 2) for t in range(1, NT - 1, 2)] + [(NT - 1, 1)]
NU = len(UNITS)
VECTOR_SCALED = 6
H_BANKS = [0, 1]
M_BANKS = [7, 2, 3, 4, 5, 6]

STORES = (["A", "B", "A", "A", "AB", "AA", "AAAB", "AAAB", "AACC", "AAAB"]
          + ["AAAB AACC", "AAAB AAAB", "AACC AAAB", "AAAB AACC"] + ["AAAB", "AAAA"])


def tile_lowrankredistributor_t_kernel(tc, logits, W, out):
    nc = tc.nc
    x_rows = logits.rearrange("(p t) v -> p t v", t=NT)
    out_rows = out.rearrange("(p t) v -> p (t v)", t=NT)
    cross = 2.0 * ALPHA * (1.0 - ALPHA)
    with ExitStack() as ctx:
        ctx.enter_context(tc.manual_schedule())
        keep = ctx.enter_context(tc.tile_pool(name="keep", bufs=1))
        psum = ctx.enter_context(tc.psum_pool(name="psum", bufs=1))

        def bank(index, shape, dtype, name):
            return psum.tile(shape, dtype, tag="b%d" % index, name=name)

        warm = keep.tile([P, 1], F32)
        nc.vector.memset(warm[:], 1.0)
        nc.scalar.activation(out=warm[:], in_=warm[:], func=ACT.Sqrt)
        ident = keep.tile([P, P], F32)
        make_identity(nc, ident[:])
        ones = keep.tile([P, P], F32)
        nc.vector.memset(ones[:], 1.0)
        norm_bias = keep.tile([P, 1], F32)
        nc.vector.tensor_scalar(out=norm_bias[:], in0=ones[:, 0:1], scalar1=0.0,
                                scalar2=1.0 + ((1.0 - ALPHA) / ALPHA) ** 2, op0=ALU.mult, op1=ALU.add)

        x_sb = keep.tile([P, NT, V], BF16)
        x_words = x_sb[:].bitcast(F32)
        w0_codes = keep.tile([P, 2 * R], U32, align_bytes=64)
        w0_scales = keep.tile([P, 2 * R], U8, align_bytes=64)
        wt_codes = keep.tile([P, V], U32, align_bytes=64)
        wt_scales = keep.tile([P, V], U8, align_bytes=64)
        h_codes = keep.tile([P, B], U32, align_bytes=64)
        h_scales = keep.tile([P, B], U8, align_bytes=64)
        sq_sums = keep.tile([P, SQ_COLS], F32)
        nc.vector.memset(sq_sums[:], 0.0)
        m_sq_sums = keep.tile([P, PIECES], F32)
        m_x_sums = keep.tile([P, PIECES], F32)
        x2_copy = keep.tile([P, SQ_COLS], F32)
        sum_x2 = keep.tile([P, 1], F32)
        l_n = keep.tile([P, 1], F32)
        inv_l_n = keep.tile([P, 1], F32)
        inv_l_n_gp = keep.tile([P, 1], F32)
        m_copy = keep.tile([P, PIECES], F32)
        m_sq = keep.tile([P, 1], F32)
        m_x = keep.tile([P, 1], F32)
        m_norm = keep.tile([P, 1], F32)
        inv_m = keep.tile([P, 1], F32)
        rho_l_n = keep.tile([P, 1], F32)
        cross_l_n = keep.tile([P, 1], F32)
        rho = keep.tile([P, 1], F32)
        o_sq = keep.tile([P, 1], F32)
        o_norm = keep.tile([P, 1], F32)
        beta = keep.tile([P, 1], F32)
        rho_beta = keep.tile([P, 1], F32)

        def x_piece(piece):
            return x_sb[:, piece // 2, (piece % 2) * BANK:(piece % 2 + 1) * BANK]

        def second_matmul(piece, index):
            t = piece // 2
            cols = slice((piece % 2) * BANK, (piece % 2 + 1) * BANK)
            minted = bank(index, [P, BANK], F32, "minted")
            nc.tensor.matmul_mx(
                out=minted[:],
                lhsT=h_codes[:, t * P:(t + 1) * P].bitcast(FP8X4),
                lhsT_scale=h_scales[:, t * P:(t + 1) * P],
                rhs=wt_codes[:, cols].bitcast(FP8X4),
                rhs_scale=wt_scales[:, cols],
                start=True, stop=True)
            return minted

        with tc.tile_pool(name="ab", bufs=1) as ab:
            w_raw = ab.tile([P, 4, 2, R], BF16)
            w_raw_words = w_raw[:].bitcast(F32)
            w_by_pass = w_raw[:].rearrange("q (g u) e r -> q g (u e) r", g=2)
            xt_words = ab.tile([P, NT, V // 2], F32, align_bytes=64)
            xt = xt_words[:].bitcast(BF16)
            w0_grouped = ab.tile([P, 2, R, 4], BF16, align_bytes=64)
            wt_grouped = ab.tile([P, V, 2], F32, align_bytes=64)

            w_rows = W.rearrange("(s q e) r -> q s e r", s=4, e=2)
            for s in range(4):
                nc.sync.dma_start(out=w_raw[:, s], in_=w_rows[:, s])
            first = 0
            for n in LOADS:
                nc.sync.dma_start(out=x_sb[:, first:first + n, :], in_=x_rows[:, first:first + n, :])
                first += n

            gram = bank(7, [P, P], F32, "gram")
            gram_tiles = [t for t in range(NT) if SQUARES[t] == "T"]
            xt_bank = {}

            def square_on_tensor(t):
                for j in range(V // P):
                    block = x_sb[:, t, j * P:(j + 1) * P]
                    nc.tensor.matmul(out=gram[:], lhsT=block, rhs=block, start=(t == gram_tiles[0] and j == 0),
                                     stop=(t == gram_tiles[-1] and j == V // P - 1))

            def square_on_scalar(t, n, col):
                squares = ab.tile([P, 2, V], BF16, bufs=2, name="squares")
                nc.scalar.activation(out=squares[:, 0:n, :], in_=x_sb[:, t:t + n, :], func=ACT.Square,
                                     accum_out=sq_sums[:, col:col + 1])

            def transpose_x(t, index):
                xt_bank[t] = bank(index, [P, 4, P], F32, "xt_bank")
                for gu in range(4):
                    nc.tensor.transpose(out=xt_bank[t][:, gu, :], in_=x_words[:, t, gu * P:(gu + 1) * P],
                                        identity=ident[:])

            def copy_out_x(t, engine):
                dst = xt_words[:, t, :].rearrange("q (g n u) -> q g n u", g=2, u=2)
                src = xt_bank[t][:].rearrange("q (g u) n -> q g n u", g=2)
                if engine == "scalar":
                    nc.scalar.copy(out=dst, in_=src)
                else:
                    nc.vector.tensor_copy(out=dst, in_=src)

            def regroup_w0(g, u2):
                nc.gpsimd.tensor_scalar(
                    out=w0_grouped[:, g, u2 * R2:(u2 + 1) * R2, :].rearrange("q (e p) y -> q e p y", e=2),
                    in0=w_by_pass[:, g, :, u2 * R2:(u2 + 1) * R2].rearrange("q y (p e) -> q e p y", e=2),
                    scalar1=1.0, scalar2=0.0, op0=ALU.mult, op1=ALU.add)

            def transpose_w(s, index):
                wt_bank = bank(index, [P, 2, 2, P], F32, "wt_bank")
                for e in range(2):
                    for u in range(2):
                        nc.tensor.transpose(out=wt_bank[:, e, u, :], in_=w_raw_words[:, s, e, u * P:(u + 1) * P],
                                            identity=ident[:])
                nc.scalar.copy(out=wt_grouped[:, s * SLAB:(s + 1) * SLAB, :].rearrange("p (q e) u -> p q e u", e=2),
                               in_=wt_bank[:].rearrange("p e u q -> p q e u"))

            turn = 0
            col = 0
            first = 0
            for s in range(4):
                transpose_w(s, turn % EARLY_BANKS)
                turn += 1
            for g in range(2):
                for u2 in range(2):
                    regroup_w0(g, u2)
            for i, n in enumerate(LOADS):
                tiles = list(range(first, first + n))
                first += n
                for t in tiles:
                    if t < EARLY:
                        transpose_x(t, turn % EARLY_BANKS)
                        turn += 1
                        copy_out_x(t, "vector")
                for t in tiles:
                    if SQUARES[t] == "T":
                        square_on_tensor(t)
                on_scalar = [t for t in tiles if SQUARES[t] == "S"]
                if on_scalar:
                    square_on_scalar(on_scalar[0], len(on_scalar), col)
                    col += 1
                if i == 5:
                    nc.vector.quantize_mx(out=w0_codes[:].bitcast(FP8X4), scales=w0_scales[:],
                                          in_=w0_grouped[:].rearrange("q g r y -> q (g r y)"))
                if i == 6:
                    nc.vector.quantize_mx(out=wt_codes[:].bitcast(FP8X4), scales=wt_scales[:],
                                          in_=wt_grouped[:].bitcast(BF16).rearrange("p v y -> p (v y)"))

            late = list(range(EARLY, NT))
            for i, t in enumerate(late[:3]):
                transpose_x(t, LATE_BANKS[i % 4])
            diagonal = ab.tile([P, P], F32)
            nc.vector.scalar_tensor_tensor(out=diagonal[:], in0=gram[:], scalar=1.0, in1=ident[:],
                                           op0=ALU.mult, op1=ALU.mult,
                                           accum_out=sq_sums[:, SQ_COLS - 1:SQ_COLS])
            copy_out_x(late[0], "vector")
            copy_out_x(late[1], "scalar")
            copy_out_x(late[2], "vector")
            x2_bank = bank(7, [P, SQ_COLS], F32, "x2_bank")
            nc.tensor.matmul(out=x2_bank[:], lhsT=ones[:], rhs=sq_sums[:], start=True, stop=True)
            for i, t in enumerate(late[3:]):
                transpose_x(t, LATE_BANKS[(i + 3) % 4])
            nc.scalar.activation(out=x2_copy[:], in_=x2_bank[:], func=ACT.Copy, accum_out=sum_x2[:])
            nc.scalar.activation(out=l_n[:], in_=sum_x2[:], func=ACT.Sqrt)
            nc.vector.reciprocal(out=inv_l_n[:], in_=l_n[:])
            waiting = late[3:]

            xs = {}
            xq = {}
            hg = {}

            def new_xs(unit):
                xs[unit] = ab.tile([P, UNITS[unit][1] * V], BF16, align_bytes=64, bufs=2, name="xs", tag="xs")

            def scale_x(unit, engine, lo=0, hi=2):
                t0, nt = UNITS[unit]
                hi = min(hi, nt)
                src = xt[:, t0 + lo:t0 + hi, :].rearrange("q t v -> q (t v)")
                dst = xs[unit][:, lo * V:hi * V]
                if engine == "gpsimd":
                    nc.gpsimd.tensor_scalar(out=dst, in0=src, scalar1=inv_l_n_gp[:, 0:1], scalar2=0.0,
                                            op0=ALU.mult, op1=ALU.add)
                else:
                    nc.vector.tensor_scalar(out=dst, in0=src, scalar1=inv_l_n[:, 0:1], scalar2=None,
                                            op0=ALU.mult)

            def quantise_x(unit):
                nt = UNITS[unit][1]
                codes = ab.tile([P, nt * TILE_WORDS], U32, align_bytes=64, bufs=3, name="xq", tag="xq")
                scales = ab.tile([P, nt * TILE_WORDS], U8, align_bytes=64, bufs=3, name="xqs", tag="xqs")
                nc.vector.quantize_mx(out=codes[:].bitcast(FP8X4), scales=scales[:], in_=xs[unit][:])
                xq[unit] = (codes, scales)

            def first_matmul(unit):
                t0, nt = UNITS[unit]
                codes, scales = xq[unit]
                hg[unit] = ab.tile([P, nt, P, 4], BF16, align_bytes=64, bufs=3, name="hg", tag="hg")
                for i in range(nt):
                    h_bank = bank(H_BANKS[(t0 + i) % 2], [P, 4, P], F32, "h_bank")
                    for y in range(4):
                        for g in range(2):
                            w_cols = slice(g * R + y * P, g * R + (y + 1) * P)
                            x_cols = slice(i * TILE_WORDS + g * P, i * TILE_WORDS + (g + 1) * P)
                            nc.tensor.matmul_mx(
                                out=h_bank[:, y, :],
                                lhsT=w0_codes[:, w_cols].bitcast(FP8X4),
                                lhsT_scale=w0_scales[:, w_cols],
                                rhs=codes[:, x_cols].bitcast(FP8X4),
                                rhs_scale=scales[:, x_cols],
                                start=(g == 0), stop=(g == 1))
                    nc.scalar.copy(out=hg[unit][:, i], in_=h_bank[:].rearrange("p y n -> p n y"))

            def quantise_h(unit):
                t0, nt = UNITS[unit]
                nc.vector.quantize_mx(out=h_codes[:, t0 * P:(t0 + nt) * P].bitcast(FP8X4),
                                      scales=h_scales[:, t0 * P:(t0 + nt) * P],
                                      in_=hg[unit][:].rearrange("p t n y -> p (t n y)"))

            def sums_of_minted(unit, pieces):
                t0, nt = UNITS[unit]
                for piece in range(2 * t0, 2 * (t0 + nt))[pieces]:
                    minted = second_matmul(piece, M_BANKS[piece % 6])
                    squares_m = ab.tile([P, BANK], BF16, bufs=2, name="squares_m")
                    nc.scalar.activation(out=squares_m[:], in_=minted[:], func=ACT.Square,
                                         accum_out=m_sq_sums[:, piece:piece + 1])
                    products = ab.tile([P, BANK], F32, bufs=2, name="products")
                    nc.vector.scalar_tensor_tensor(out=products[:], in0=minted[:], scalar=1.0, in1=x_piece(piece),
                                                   op0=ALU.mult, op1=ALU.mult,
                                                   accum_out=m_x_sums[:, piece:piece + 1])

            new_xs(0)
            scale_x(0, "vector")
            new_xs(1)
            scale_x(1, "vector", 0, 1)
            quantise_x(0)
            scale_x(1, "vector", 1, 2)
            for i in range(-3, NU):
                if 2 <= i + 4 < VECTOR_SCALED:
                    new_xs(i + 4)
                    scale_x(i + 4, "vector")
                if VECTOR_SCALED <= i + 5 < NU:
                    new_xs(i + 5)
                if 1 <= i + 3 < NU:
                    quantise_x(i + 3)
                if i + 5 == VECTOR_SCALED:
                    nc.vector.tensor_copy(out=inv_l_n_gp[:], in_=inv_l_n[:])
                if 0 <= i + 1 < NU:
                    quantise_h(i + 1)
                if VECTOR_SCALED <= i + 5 < NU:
                    scale_x(i + 5, "gpsimd")
                if i + 5 == VECTOR_SCALED:
                    nc.gpsimd.tensor_scalar(out=rho_l_n[:], in0=l_n[:], scalar1=(1.0 - ALPHA) / ALPHA, scalar2=0.0,
                                            op0=ALU.mult, op1=ALU.add)
                    nc.gpsimd.tensor_scalar(out=cross_l_n[:], in0=inv_l_n[:], scalar1=cross, scalar2=0.0,
                                            op0=ALU.mult, op1=ALU.add)
                if i >= 0:
                    sums_of_minted(i, slice(0, 3))
                if 0 <= i + 2 < NU:
                    first_matmul(i + 2)
                if i >= 0:
                    sums_of_minted(i, slice(3, None))
                for t in waiting[:4]:
                    copy_out_x(t, "scalar")
                waiting = waiting[4:]

        m_sq_bank = bank(0, [P, PIECES], F32, "m_sq_bank")
        m_x_bank = bank(1, [P, PIECES], F32, "m_x_bank")
        last = 2 * UNITS[-1][0]
        for pieces in (slice(0, last), slice(last, PIECES)):
            for sums_bank, sums in ((m_sq_bank, m_sq_sums), (m_x_bank, m_x_sums)):
                nc.tensor.matmul(out=sums_bank[:, pieces], lhsT=ones[:], rhs=sums[:, pieces], start=True, stop=True)
        nc.scalar.activation(out=m_copy[:], in_=m_sq_bank[:], func=ACT.Copy, accum_out=m_sq[:])
        nc.scalar.activation(out=m_norm[:], in_=m_sq[:], func=ACT.Sqrt)
        nc.vector.reciprocal(out=inv_m[:], in_=m_norm[:])
        nc.vector.tensor_scalar(out=rho[:], in0=inv_m[:], scalar1=rho_l_n[:, 0:1], scalar2=None, op0=ALU.mult)
        nc.vector.reduce_sum(out=m_x[:], in_=m_x_bank[:], axis=AX.X)
        nc.vector.scalar_tensor_tensor(out=o_sq[:], in0=m_x[:], scalar=inv_m[:, 0:1], in1=cross_l_n[:],
                                       op0=ALU.mult, op1=ALU.mult)
        nc.scalar.activation(out=o_norm[:], in_=o_sq[:], func=ACT.Sqrt, bias=norm_bias[:, 0:1],
                             scale=1.0 / (ALPHA * ALPHA))

        with tc.tile_pool(name="cc", bufs=1) as cc:
            first = 0
            for groups in STORES:
                n_pieces = len(groups.replace(" ", ""))
                stage = cc.tile([P, n_pieces * BANK], F32, bufs=7, name="stage", tag="stage")
                start = 0
                for ways in groups.split(" "):
                    for i, way in enumerate(ways):
                        piece = first + start + i
                        cols = slice((start + i) * BANK, (start + i + 1) * BANK)
                        minted = second_matmul(piece, (piece + 2) % 8)
                        if way != "B":
                            nc.vector.scalar_tensor_tensor(out=stage[:, cols], in0=minted[:], scalar=rho[:, 0:1],
                                                           in1=x_piece(piece), op0=ALU.mult, op1=ALU.add)
                            if piece == 0:
                                nc.vector.reciprocal(out=beta[:], in_=o_norm[:])
                                nc.vector.tensor_scalar(out=rho_beta[:], in0=rho[:], scalar1=beta[:, 0:1], scalar2=None,
                                                        op0=ALU.mult)
                                nc.vector.tensor_scalar(out=stage[:, cols], in0=stage[:, cols], scalar1=beta[:, 0:1],
                                                        scalar2=None, op0=ALU.mult)
                        else:
                            beta_logits = cc.tile([P, BANK], F32, bufs=3, name="beta_logits", tag="beta_logits")
                            nc.gpsimd.tensor_scalar(out=beta_logits[:], in0=x_piece(piece), scalar1=beta[:, 0:1],
                                                    scalar2=0.0, op0=ALU.mult, op1=ALU.add)
                            nc.scalar.activation(out=stage[:, cols], in_=minted[:], func=ACT.Copy,
                                                 scale=rho_beta[:, 0:1])
                            nc.gpsimd.tensor_tensor(out=stage[:, cols], in0=stage[:, cols], in1=beta_logits[:],
                                                    op=ALU.add)
                    if "A" in ways and first + start > 0:
                        on_scalar = slice(start * BANK, (start + ways.count("A")) * BANK)
                        nc.scalar.activation(out=stage[:, on_scalar], in_=stage[:, on_scalar], func=ACT.Copy,
                                             scale=beta[:, 0:1])
                    if "C" in ways:
                        on_gpsimd = slice((start + ways.index("C")) * BANK, (start + len(ways)) * BANK)
                        nc.gpsimd.tensor_scalar(out=stage[:, on_gpsimd], in0=stage[:, on_gpsimd], scalar1=beta[:, 0:1],
                                                scalar2=0.0, op0=ALU.mult, op1=ALU.add)
                    start += len(ways)
                nc.sync.dma_start(out=out_rows[:, first * BANK:(first + n_pieces) * BANK], in_=stage[:])
                first += n_pieces
